import numpy as np
import ml_dtypes


def mxq(x, axis, fmt="e4m3"):
    dtype, down = {"e4m3": (ml_dtypes.float8_e4m3fn, 7), "e5m2": (ml_dtypes.float8_e5m2, 14)}[fmt]
    v = np.moveaxis(np.asarray(x, np.float32).astype(ml_dtypes.bfloat16).astype(np.float64), axis, -1)
    blocks = v.reshape(v.shape[:-1] + (-1, 32))
    amax = np.abs(blocks).max(-1, keepdims=True)
    byte = np.maximum(np.where(amax > 0, np.frexp(amax)[1] - 1 + 127, 0) - down, 1)
    scale = np.exp2(byte - 127.0)
    codes = (blocks / scale).astype(np.float32).astype(dtype).astype(np.float64)
    return np.moveaxis((codes * scale).reshape(v.shape), -1, axis)


WIDE = False


def mx_kscale(k):
    if not WIDE:
        return np.ones(k)
    levels = np.array([10, -10, 5, -5, 0])
    a = np.random.permutation(np.resize(levels, k // 512 * 4)).reshape(k // 512, 4)
    idx = np.arange(k)
    return np.exp2(a[idx // 512, idx % 128 // 32])


BF16 = ml_dtypes.bfloat16


def bf(x):
    return np.asarray(x, np.float32).astype(BF16)


def f64(x):
    return np.asarray(x).astype(np.float64)


N, D, HOP = 1024, 512, 2
NW = sum(range(HOP + 1))


def setup_inputs():
    s = mx_kscale(N)
    u = s / s.min()
    g = u[None, :] / u[:, None]
    return {"A_p": bf(np.random.standard_normal((N, N)) / np.sqrt(N) * g),
            "A_n": bf(np.random.standard_normal((N, N)) / np.sqrt(N) * g),
            "x_n": bf(np.random.standard_normal((N, D)) / u[:, None]),
            "w_n": bf(1.0 + 0.1 * np.random.standard_normal((NW, 1)))}


def reference(A_p, A_n, x_n, w_n):
    ap = mxq(f64(A_p), 1, "e4m3")
    an = mxq(f64(A_n), 1, "e4m3")
    xq = mxq(f64(x_n), 0, "e4m3")
    wa, wb, wc = f64(w_n)
    n1 = an @ xq
    feat_n = wa * n1
    feat_n = feat_n + wb * (ap @ mxq(n1, 0, "e4m3"))
    p1 = ap @ xq
    feat_n = feat_n + wc * (an @ mxq(p1, 0, "e4m3"))
    return feat_n

@@ -1,0 +1,266 @@
+from contextlib import ExitStack
+
+import concourse.mybir as mybir
+from concourse.masks import make_identity
+
+F32 = mybir.dt.float32
+BF16 = mybir.dt.bfloat16
+U32 = mybir.dt.uint32
+U8 = mybir.dt.uint8
+FP8X4 = mybir.dt.float8_e4m3fn_x4
+MULT = mybir.AluOpType.mult
+ADD = mybir.AluOpType.add
+COPY = mybir.ActivationFunctionType.Copy
+
+P = 128
+N = 1024
+D = 512
+FLOPS = 4 * 2 * N * N * D
+
+MANUAL = True
+X_SPLIT = 88
+C_ORDER = (0, 3, 1, 2)
+C_ENG = {0: "sv", 1: "sv", 2: "ss", 3: "ss", 4: "ss", 5: "ss", 6: "ss", 7: "ss"}
+EP_ENG = "sssv"
+EN_ENG = ("ssvv", "ssvv")
+S2_Y = ()
+S1_Y = ()
+
+
+def tile_simpa_pa_kernel(tc, A_p, A_n, x_n, w_n, out):
+    nc = tc.nc
+    with ExitStack() as ctx:
+        keep = ctx.enter_context(tc.tile_pool(name="keep", bufs=1))
+        psum = ctx.enter_context(tc.psum_pool(name="psum", bufs=4))
+        if MANUAL:
+            ctx.enter_context(tc.manual_schedule())
+
+        def copy_on(eng, dst, src):
+            if eng == "v":
+                nc.vector.tensor_copy(out=dst, in_=src)
+            else:
+                nc.scalar.copy(out=dst, in_=src)
+
+        ident = keep.tile([P, P], F32, name="ident")
+        make_identity(nc, ident[:])
+        w_bf = keep.tile([P, 3], BF16, name="w_bf")
+        nc.scalar.dma_start(out=w_bf[:], in_=w_n.rearrange("a b -> (a b)").partition_broadcast(P))
+        w_f = keep.tile([P, 3], F32, name="w_f")
+
+        x_raw = keep.tile([P, 4096], BF16, name="x_raw")
+        x_src = x_n.rearrange("(a p e) d -> p a (e d)", a=4, p=P, e=2)
+        x_dst = x_raw[:].rearrange("p (a f) -> p a f", a=4)
+        for kg in range(2):
+            nc.sync.dma_start(out=x_dst[:, 2 * kg:2 * kg + 2, :], in_=x_src[:, 2 * kg:2 * kg + 2, :])
+        a_raw = []
+        for k in range(8):
+            src = (A_p, A_n)[k // 4].rearrange("(a p e) j -> a p (e j)", a=4, p=P, e=2)
+            raw = keep.tile([P, 2048], BF16, name="a_raw%d" % k)
+            nc.sync.dma_start(out=raw[:], in_=src[k % 4])
+            a_raw.append(raw)
+
+        nc.scalar.activation(out=w_f[:], in_=w_bf[:], func=COPY)
+        wa = w_f[:, 0:1]
+        wb = w_f[:, 1:2]
+        wc = w_f[:, 2:3]
+
+        x_grp = keep.tile([P, 4096], BF16, name="x_grp", align_bytes=64)
+        x_cod = keep.tile([P, 1024], U32, name="x_cod", align_bytes=64)
+        x_scl = keep.tile([P, 1024], U8, name="x_scl", align_bytes=64)
+        for kg in range(2):
+            dst = x_grp[:, kg * 2048:(kg + 1) * 2048].rearrange("p (c i t) -> p c t i", i=4, t=4)
+            src = x_raw[:, kg * 2048:(kg + 1) * 2048].rearrange("p (t c i) -> p c t i", t=4, i=4)
+            copy_on("v", dst[:, 0:X_SPLIT], src[:, 0:X_SPLIT])
+            copy_on("s", dst[:, X_SPLIT:128], src[:, X_SPLIT:128])
+        for kg in range(2):
+            nc.vector.quantize_mx(
+                out=x_cod[:, kg * 512:(kg + 1) * 512].bitcast(FP8X4),
+                scales=x_scl[:, kg * 512:(kg + 1) * 512],
+                in_=x_grp[:, kg * 2048:(kg + 1) * 2048],
+            )
+
+        a_cod = [keep.tile([P, 2048], U32, name="a_cod%d" % m, align_bytes=64) for m in range(2)]
+        a_scl = [keep.tile([P, 2048], U8, name="a_scl%d" % m, align_bytes=64) for m in range(2)]
+        h_grp = [keep.tile([P, 4096], BF16, name="h_grp%d" % m, align_bytes=64) for m in range(2)]
+        h_cod = [keep.tile([P, 1024], U32, name="h_cod%d" % m, align_bytes=64) for m in range(2)]
+        h_scl = [keep.tile([P, 1024], U8, name="h_scl%d" % m, align_bytes=64) for m in range(2)]
+        t_n = keep.tile([P, 4096], F32, name="t_n")
+        acc = keep.tile([P, 4096], F32, name="acc")
+        o_sb = keep.tile([P, 4096], F32, name="o_sb")
+        out_v = out.rearrange("(a p e) d -> a e p d", a=4, p=P, e=2)
+
+        t_bank = {}
+        a_grp = {}
+        m_bank = {}
+
+        def transposes(k):
+            words = a_raw[k][:].bitcast(F32)
+            for e in range(2):
+                bank = psum.tile([P, 512], F32, tag="ts", name="tb%d%d" % (k, e))
+                for s in range(4):
+                    nc.tensor.transpose(
+                        bank[:, s * P:(s + 1) * P],
+                        words[:, e * 512 + s * P:e * 512 + (s + 1) * P],
+                        ident[:],
+                    )
+                t_bank[(k, e)] = bank
+
+        def copies(k):
+            grp = keep.tile([P, 2048], BF16, name="a_grp%d" % k, align_bytes=64)
+            a_grp[k] = grp
+            words = grp[:].bitcast(F32)
+            for e in range(2):
+                copy_on(
+                    C_ENG[k][e],
+                    words[:, e * 512:(e + 1) * 512].rearrange("p (k i u) -> p k i u", k=2, i=P, u=2),
+                    t_bank[(k, e)][:].rearrange("p (k u i) -> p k i u", k=2, u=2, i=P),
+                )
+
+        def quantise_a(k):
+            m, a = k // 4, k % 4
+            nc.vector.quantize_mx(
+                out=a_cod[m][:, a * 512:(a + 1) * 512].bitcast(FP8X4),
+                scales=a_scl[m][:, a * 512:(a + 1) * 512],
+                in_=a_grp[k][:],
+            )
+
+        def mx(dst, m, r, kg, cod, scl, lo, hi):
+            w0 = r * 256 + kg * P
+            nc.tensor.matmul_mx(
+                out=dst,
+                lhsT=a_cod[m][:, w0:w0 + P].bitcast(FP8X4),
+                lhsT_scale=a_scl[m][:, w0:w0 + P],
+                rhs=cod[:, kg * 512 + lo:kg * 512 + hi].bitcast(FP8X4),
+                rhs_scale=scl[:, kg * 512 + lo:kg * 512 + hi],
+                start=(kg == 0),
+                stop=(kg == 1),
+            )
+
+        def first_hop(k):
+            m, a = k // 4, k % 4
+            g = a // 2
+            if a % 2 == 0:
+                for c in range(4):
+                    m_bank[(m, g, c)] = psum.tile([P, 512], F32, tag="mm", name="mb%d%d%d" % (m, g, c))
+            for c in C_ORDER:
+                for e in range(2):
+                    r = 2 * a + e
+                    t = r % 4
+                    for kg in range(2):
+                        mx(m_bank[(m, g, c)][:, t * P:(t + 1) * P], m, r, kg, x_cod, x_scl, c * P, (c + 1) * P)
+
+        def regroup(eng, m, g, c):
+            lo = g * 2048 + c * 512
+            copy_on(
+                eng,
+                h_grp[m][:, lo:lo + 512].rearrange("p (d t) -> p d t", t=4),
+                m_bank[(m, g, c)][:].rearrange("p (t d) -> p d t", t=4),
+            )
+
+        def scaled(eng, g, c):
+            dst = t_n[:, g * 2048:(g + 1) * 2048].rearrange("p (t c d) -> p t c d", t=4, c=4)[:, :, c, :]
+            src = m_bank[(1, g, c)][:].rearrange("p (t d) -> p t d", t=4)
+            if eng == "v":
+                nc.vector.tensor_scalar(out=dst, in0=src, scalar1=wa, scalar2=None, op0=MULT)
+            else:
+                nc.scalar.activation(out=dst, in_=src, func=COPY, scale=wa)
+
+        def quantise_h(m, g):
+            nc.vector.quantize_mx(
+                out=h_cod[m][:, g * 512:(g + 1) * 512].bitcast(FP8X4),
+                scales=h_scl[m][:, g * 512:(g + 1) * 512],
+                in_=h_grp[m][:, g * 2048:(g + 1) * 2048],
+            )
+
+        def evac_p(g):
+            for c in C_ORDER:
+                regroup(EP_ENG[c], 0, g, c)
+
+        def evac_n(g):
+            if g == 0:
+                for c in C_ORDER:
+                    regroup(EN_ENG[g][c], 1, g, c)
+                    scaled(EN_ENG[g][c], g, c)
+                quantise_h(1, g)
+            else:
+                for c in C_ORDER:
+                    regroup(EN_ENG[g][c], 1, g, c)
+                scaled(EN_ENG[g][3], g, 3)
+                quantise_h(1, g)
+                for c in (0, 1, 2):
+                    scaled(EN_ENG[g][c], g, c)
+
+        def second_hop(m, a, tag, weight, base, dst, slow, store):
+            other = 1 - m
+            banks = []
+            for e in range(2):
+                r = 2 * a + e
+                bank = psum.tile([P, 512], F32, tag=tag, name="sb%d%d" % (m, r))
+                for kg in range(2):
+                    mx(bank[:], m, r, kg, h_cod[other], h_scl[other], 0, 512)
+                banks.append(bank)
+            for e in range(2):
+                r = 2 * a + e
+                if r in slow:
+                    cols = slice(r * 512, (r + 1) * 512)
+                    tmp = keep.tile([P, 512], F32, name="tmp%d%d" % (m, r))
+                    nc.scalar.activation(out=tmp[:], in_=banks[e][:], func=COPY, scale=weight)
+                    nc.gpsimd.tensor_tensor(out=dst[:, cols], in0=tmp[:], in1=base[:, cols], op=ADD)
+                    if store:
+                        nc.sync.dma_start(out=out_v[a, e], in_=dst[:, cols])
+                else:
+                    pieces = 2 if (store and r == 7) else 1
+                    width = 512 // pieces
+                    for h in range(pieces):
+                        cols = slice(r * 512 + h * width, r * 512 + (h + 1) * width)
+                        nc.vector.scalar_tensor_tensor(
+                            out=dst[:, cols], in0=banks[e][:, h * width:(h + 1) * width], scalar=weight,
+                            in1=base[:, cols], op0=MULT, op1=ADD
+                        )
+                        if store:
+                            nc.sync.dma_start(out=out_v[a, e][:, h * width:(h + 1) * width], in_=dst[:, cols])
+
+        transposes(0)
+        copies(0)
+        transposes(1)
+        copies(1)
+        quantise_a(0)
+        transposes(2)
+        copies(2)
+        quantise_a(1)
+        first_hop(0)
+        transposes(3)
+        copies(3)
+        quantise_a(2)
+        first_hop(1)
+        evac_p(0)
+        quantise_a(3)
+        quantise_h(0, 0)
+        transposes(4)
+        copies(4)
+        transposes(5)
+        copies(5)
+        first_hop(2)
+        quantise_a(4)
+        first_hop(3)
+        evac_p(1)
+        quantise_a(5)
+        quantise_h(0, 1)
+        transposes(6)
+        copies(6)
+        transposes(7)
+        copies(7)
+        first_hop(4)
+        quantise_a(6)
+        first_hop(5)
+        quantise_a(7)
+        evac_n(0)
+        second_hop(1, 0, "ts", wc, t_n, acc, S2_Y, False)
+        second_hop(1, 1, "ts", wc, t_n, acc, S2_Y, False)
+        first_hop(6)
+        first_hop(7)
+        evac_n(1)
+        second_hop(1, 2, "ts", wc, t_n, acc, S2_Y, False)
+        second_hop(1, 3, "ts", wc, t_n, acc, S2_Y, False)
+        for a in range(4):
+            second_hop(0, a, "mm" if a < 2 else "ts", wb, acc, o_sb, S1_Y, True)

@@ -23,7 +23,7 @@ C_ORDER = (0, 3, 1, 2)
 C_ENG = {0: "sv", 1: "sv", 2: "ss", 3: "ss", 4: "ss", 5: "ss", 6: "ss", 7: "ss"}
 EP_ENG = "sssv"
 EN_ENG = ("ssvv", "ssvv")
-S2_Y = ()
+S2_Y = (0, 1, 2, 3, 4, 5, 6, 7)
 S1_Y = ()
 
 

@@ -16,15 +16,7 @@ P = 128
 N = 1024
 D = 512
 FLOPS = 4 * 2 * N * N * D
-
-MANUAL = True
 X_SPLIT = 88
-C_ORDER = (0, 3, 1, 2)
-C_ENG = {0: "sv", 1: "sv", 2: "ss", 3: "ss", 4: "ss", 5: "ss", 6: "ss", 7: "ss"}
-EP_ENG = "sssv"
-EN_ENG = ("ssvv", "ssvv")
-S2_Y = (0, 1, 2, 3, 4, 5, 6, 7)
-S1_Y = ()
 
 
 def tile_simpa_pa_kernel(tc, A_p, A_n, x_n, w_n, out):
@@ -32,11 +24,10 @@ def tile_simpa_pa_kernel(tc, A_p, A_n, x_n, w_n, out):
     with ExitStack() as ctx:
         keep = ctx.enter_context(tc.tile_pool(name="keep", bufs=1))
         psum = ctx.enter_context(tc.psum_pool(name="psum", bufs=4))
-        if MANUAL:
-            ctx.enter_context(tc.manual_schedule())
+        ctx.enter_context(tc.manual_schedule())
 
-        def copy_on(eng, dst, src):
-            if eng == "v":
+        def copy_on(on_vector, dst, src):
+            if on_vector:
                 nc.vector.tensor_copy(out=dst, in_=src)
             else:
                 nc.scalar.copy(out=dst, in_=src)
@@ -45,7 +36,6 @@ def tile_simpa_pa_kernel(tc, A_p, A_n, x_n, w_n, out):
         make_identity(nc, ident[:])
         w_bf = keep.tile([P, 3], BF16, name="w_bf")
         nc.scalar.dma_start(out=w_bf[:], in_=w_n.rearrange("a b -> (a b)").partition_broadcast(P))
-        w_f = keep.tile([P, 3], F32, name="w_f")
 
         x_raw = keep.tile([P, 4096], BF16, name="x_raw")
         x_src = x_n.rearrange("(a p e) d -> p a (e d)", a=4, p=P, e=2)
@@ -54,11 +44,12 @@ def tile_simpa_pa_kernel(tc, A_p, A_n, x_n, w_n, out):
             nc.sync.dma_start(out=x_dst[:, 2 * kg:2 * kg + 2, :], in_=x_src[:, 2 * kg:2 * kg + 2, :])
         a_raw = []
         for k in range(8):
-            src = (A_p, A_n)[k // 4].rearrange("(a p e) j -> a p (e j)", a=4, p=P, e=2)
+            src = (A_n, A_p)[k // 4].rearrange("(a p e) j -> a p (e j)", a=4, p=P, e=2)
             raw = keep.tile([P, 2048], BF16, name="a_raw%d" % k)
             nc.sync.dma_start(out=raw[:], in_=src[k % 4])
             a_raw.append(raw)
 
+        w_f = keep.tile([P, 3], F32, name="w_f")
         nc.scalar.activation(out=w_f[:], in_=w_bf[:], func=COPY)
         wa = w_f[:, 0:1]
         wb = w_f[:, 1:2]
@@ -70,8 +61,8 @@ def tile_simpa_pa_kernel(tc, A_p, A_n, x_n, w_n, out):
         for kg in range(2):
             dst = x_grp[:, kg * 2048:(kg + 1) * 2048].rearrange("p (c i t) -> p c t i", i=4, t=4)
             src = x_raw[:, kg * 2048:(kg + 1) * 2048].rearrange("p (t c i) -> p c t i", t=4, i=4)
-            copy_on("v", dst[:, 0:X_SPLIT], src[:, 0:X_SPLIT])
-            copy_on("s", dst[:, X_SPLIT:128], src[:, X_SPLIT:128])
+            copy_on(True, dst[:, 0:X_SPLIT], src[:, 0:X_SPLIT])
+            copy_on(False, dst[:, X_SPLIT:128], src[:, X_SPLIT:128])
         for kg in range(2):
             nc.vector.quantize_mx(
                 out=x_cod[:, kg * 512:(kg + 1) * 512].bitcast(FP8X4),
@@ -84,17 +75,15 @@ def tile_simpa_pa_kernel(tc, A_p, A_n, x_n, w_n, out):
         h_grp = [keep.tile([P, 4096], BF16, name="h_grp%d" % m, align_bytes=64) for m in range(2)]
         h_cod = [keep.tile([P, 1024], U32, name="h_cod%d" % m, align_bytes=64) for m in range(2)]
         h_scl = [keep.tile([P, 1024], U8, name="h_scl%d" % m, align_bytes=64) for m in range(2)]
-        t_n = keep.tile([P, 4096], F32, name="t_n")
         acc = keep.tile([P, 4096], F32, name="acc")
-        o_sb = keep.tile([P, 4096], F32, name="o_sb")
         out_v = out.rearrange("(a p e) d -> a e p d", a=4, p=P, e=2)
-
-        t_bank = {}
         a_grp = {}
-        m_bank = {}
 
-        def transposes(k):
+        def transpose_pair(k):
             words = a_raw[k][:].bitcast(F32)
+            grp = keep.tile([P, 2048], BF16, name="a_grp%d" % k, align_bytes=64)
+            a_grp[k] = grp
+            grp_words = grp[:].bitcast(F32)
             for e in range(2):
                 bank = psum.tile([P, 512], F32, tag="ts", name="tb%d%d" % (k, e))
                 for s in range(4):
@@ -103,20 +92,12 @@ def tile_simpa_pa_kernel(tc, A_p, A_n, x_n, w_n, out):
                         words[:, e * 512 + s * P:e * 512 + (s + 1) * P],
                         ident[:],
                     )
-                t_bank[(k, e)] = bank
-
-        def copies(k):
-            grp = keep.tile([P, 2048], BF16, name="a_grp%d" % k, align_bytes=64)
-            a_grp[k] = grp
-            words = grp[:].bitcast(F32)
-            for e in range(2):
-                copy_on(
-                    C_ENG[k][e],
-                    words[:, e * 512:(e + 1) * 512].rearrange("p (k i u) -> p k i u", k=2, i=P, u=2),
-                    t_bank[(k, e)][:].rearrange("p (k u i) -> p k i u", k=2, u=2, i=P),
+                nc.scalar.copy(
+                    out=grp_words[:, e * 512:(e + 1) * 512].rearrange("p (k i u) -> p k i u", k=2, i=P, u=2),
+                    in_=bank[:].rearrange("p (k u i) -> p k i u", k=2, u=2, i=P),
                 )
 
-        def quantise_a(k):
+        def quantise_pair(k):
             m, a = k // 4, k % 4
             nc.vector.quantize_mx(
                 out=a_cod[m][:, a * 512:(a + 1) * 512].bitcast(FP8X4),
@@ -136,131 +117,75 @@ def tile_simpa_pa_kernel(tc, A_p, A_n, x_n, w_n, out):
                 stop=(kg == 1),
             )
 
-        def first_hop(k):
-            m, a = k // 4, k % 4
-            g = a // 2
-            if a % 2 == 0:
+        def first_hop(m, g):
+            banks = [psum.tile([P, 512], F32, tag="mm", name="mb%d%d%d" % (m, g, c)) for c in range(4)]
+            for half in range(2):
                 for c in range(4):
-                    m_bank[(m, g, c)] = psum.tile([P, 512], F32, tag="mm", name="mb%d%d%d" % (m, g, c))
-            for c in C_ORDER:
-                for e in range(2):
-                    r = 2 * a + e
-                    t = r % 4
-                    for kg in range(2):
-                        mx(m_bank[(m, g, c)][:, t * P:(t + 1) * P], m, r, kg, x_cod, x_scl, c * P, (c + 1) * P)
+                    for t in (2 * half, 2 * half + 1):
+                        for kg in range(2):
+                            mx(banks[c][:, t * P:(t + 1) * P], m, 4 * g + t, kg, x_cod, x_scl, c * P, (c + 1) * P)
+            return banks
 
-        def regroup(eng, m, g, c):
-            lo = g * 2048 + c * 512
-            copy_on(
-                eng,
-                h_grp[m][:, lo:lo + 512].rearrange("p (d t) -> p d t", t=4),
-                m_bank[(m, g, c)][:].rearrange("p (t d) -> p d t", t=4),
-            )
-
-        def scaled(eng, g, c):
-            dst = t_n[:, g * 2048:(g + 1) * 2048].rearrange("p (t c d) -> p t c d", t=4, c=4)[:, :, c, :]
-            src = m_bank[(1, g, c)][:].rearrange("p (t d) -> p t d", t=4)
-            if eng == "v":
-                nc.vector.tensor_scalar(out=dst, in0=src, scalar1=wa, scalar2=None, op0=MULT)
-            else:
-                nc.scalar.activation(out=dst, in_=src, func=COPY, scale=wa)
-
-        def quantise_h(m, g):
+        def evacuate(m, g, banks):
+            for c in range(4):
+                lo = g * 2048 + c * 512
+                on_vector = c % 2 == 1
+                copy_on(
+                    on_vector,
+                    h_grp[m][:, lo:lo + 512].rearrange("p (d t) -> p d t", t=4),
+                    banks[c][:].rearrange("p (t d) -> p d t", t=4),
+                )
+                if m == 0:
+                    dst = acc[:, g * 2048:(g + 1) * 2048].rearrange("p (t c d) -> p t c d", t=4, c=4)[:, :, c, :]
+                    src = banks[c][:].rearrange("p (t d) -> p t d", t=4)
+                    if on_vector:
+                        nc.vector.tensor_scalar(out=dst, in0=src, scalar1=wa, scalar2=None, op0=MULT)
+                    else:
+                        nc.scalar.activation(out=dst, in_=src, func=COPY, scale=wa)
             nc.vector.quantize_mx(
                 out=h_cod[m][:, g * 512:(g + 1) * 512].bitcast(FP8X4),
                 scales=h_scl[m][:, g * 512:(g + 1) * 512],
                 in_=h_grp[m][:, g * 2048:(g + 1) * 2048],
             )
 
-        def evac_p(g):
-            for c in C_ORDER:
-                regroup(EP_ENG[c], 0, g, c)
-
-        def evac_n(g):
-            if g == 0:
-                for c in C_ORDER:
-                    regroup(EN_ENG[g][c], 1, g, c)
-                    scaled(EN_ENG[g][c], g, c)
-                quantise_h(1, g)
-            else:
-                for c in C_ORDER:
-                    regroup(EN_ENG[g][c], 1, g, c)
-                scaled(EN_ENG[g][3], g, 3)
-                quantise_h(1, g)
-                for c in (0, 1, 2):
-                    scaled(EN_ENG[g][c], g, c)
-
-        def second_hop(m, a, tag, weight, base, dst, slow, store):
-            other = 1 - m
+        def second_hop(m, a, tag, weight, last):
             banks = []
             for e in range(2):
-                r = 2 * a + e
-                bank = psum.tile([P, 512], F32, tag=tag, name="sb%d%d" % (m, r))
+                bank = psum.tile([P, 512], F32, tag=tag, name="sb%d%d%d" % (m, a, e))
                 for kg in range(2):
-                    mx(bank[:], m, r, kg, h_cod[other], h_scl[other], 0, 512)
+                    mx(bank[:], m, 2 * a + e, kg, h_cod[1 - m], h_scl[1 - m], 0, 512)
                 banks.append(bank)
             for e in range(2):
-                r = 2 * a + e
-                if r in slow:
-                    cols = slice(r * 512, (r + 1) * 512)
-                    tmp = keep.tile([P, 512], F32, name="tmp%d%d" % (m, r))
+                mine = acc[:, (2 * a + e) * 512:(2 * a + e + 1) * 512]
+                if e == 0 and not last:
+                    tmp = keep.tile([P, 512], F32, name="tmp%d" % a)
                     nc.scalar.activation(out=tmp[:], in_=banks[e][:], func=COPY, scale=weight)
-                    nc.gpsimd.tensor_tensor(out=dst[:, cols], in0=tmp[:], in1=base[:, cols], op=ADD)
-                    if store:
-                        nc.sync.dma_start(out=out_v[a, e], in_=dst[:, cols])
+                    nc.gpsimd.tensor_tensor(out=mine, in0=tmp[:], in1=mine, op=ADD)
                 else:
-                    pieces = 2 if (store and r == 7) else 1
-                    width = 512 // pieces
-                    for h in range(pieces):
-                        cols = slice(r * 512 + h * width, r * 512 + (h + 1) * width)
-                        nc.vector.scalar_tensor_tensor(
-                            out=dst[:, cols], in0=banks[e][:, h * width:(h + 1) * width], scalar=weight,
-                            in1=base[:, cols], op0=MULT, op1=ADD
-                        )
-                        if store:
-                            nc.sync.dma_start(out=out_v[a, e][:, h * width:(h + 1) * width], in_=dst[:, cols])
+                    nc.vector.scalar_tensor_tensor(
+                        out=mine, in0=banks[e][:], scalar=weight, in1=mine, op0=MULT, op1=ADD
+                    )
+                if last:
+                    nc.sync.dma_start(out=out_v[a, e], in_=mine)
 
-        transposes(0)
-        copies(0)
-        transposes(1)
-        copies(1)
-        quantise_a(0)
-        transposes(2)
-        copies(2)
-        quantise_a(1)
-        first_hop(0)
-        transposes(3)
-        copies(3)
-        quantise_a(2)
-        first_hop(1)
-        evac_p(0)
-        quantise_a(3)
-        quantise_h(0, 0)
-        transposes(4)
-        copies(4)
-        transposes(5)
-        copies(5)
-        first_hop(2)
-        quantise_a(4)
-        first_hop(3)
-        evac_p(1)
-        quantise_a(5)
-        quantise_h(0, 1)
-        transposes(6)
-        copies(6)
-        transposes(7)
-        copies(7)
-        first_hop(4)
-        quantise_a(6)
-        first_hop(5)
-        quantise_a(7)
-        evac_n(0)
-        second_hop(1, 0, "ts", wc, t_n, acc, S2_Y, False)
-        second_hop(1, 1, "ts", wc, t_n, acc, S2_Y, False)
-        first_hop(6)
-        first_hop(7)
-        evac_n(1)
-        second_hop(1, 2, "ts", wc, t_n, acc, S2_Y, False)
-        second_hop(1, 3, "ts", wc, t_n, acc, S2_Y, False)
+        for k in (0, 1):
+            transpose_pair(k)
+        for k in (0, 1):
+            quantise_pair(k)
+        for i in range(4):
+            m, g = i // 2, i % 2
+            if i < 3:
+                for k in (2 * i + 2, 2 * i + 3):
+                    transpose_pair(k)
+            else:
+                second_hop(1, 0, "ts", wb, False)
+                second_hop(1, 1, "ts", wb, False)
+            banks = first_hop(m, g)
+            if i < 3:
+                for k in (2 * i + 2, 2 * i + 3):
+                    quantise_pair(k)
+            evacuate(m, g, banks)
+        second_hop(1, 2, "ts", wb, False)
+        second_hop(1, 3, "ts", wb, False)
         for a in range(4):
-            second_hop(0, a, "mm" if a < 2 else "ts", wb, acc, o_sb, S1_Y, True)
+            second_hop(0, a, "mm" if a < 2 else "ts", wc, True)

@@ -17,6 +17,7 @@ N = 1024
 D = 512
 FLOPS = 4 * 2 * N * N * D
 X_SPLIT = 88
+WARM_HEAD = 14
 
 
 def tile_simpa_pa_kernel(tc, A_p, A_n, x_n, w_n, out):
@@ -31,6 +32,16 @@ def tile_simpa_pa_kernel(tc, A_p, A_n, x_n, w_n, out):
                 nc.vector.tensor_copy(out=dst, in_=src)
             else:
                 nc.scalar.copy(out=dst, in_=src)
+
+        zeros = keep.tile([P, 512], BF16, name="zeros")
+        nc.vector.memset(zeros[:], 0.0)
+        warm = psum.tile([P, 512], F32, tag="mm", name="warm")
+
+        def keep_busy(times):
+            for i in range(times):
+                nc.tensor.matmul(out=warm[:], lhsT=zeros[:, 0:P], rhs=zeros[:], start=True, stop=True)
+
+        keep_busy(WARM_HEAD)
 
         ident = keep.tile([P, P], F32, name="ident")
         make_identity(nc, ident[:])
@@ -96,6 +107,8 @@ def tile_simpa_pa_kernel(tc, A_p, A_n, x_n, w_n, out):
                     out=grp_words[:, e * 512:(e + 1) * 512].rearrange("p (k i u) -> p k i u", k=2, i=P, u=2),
                     in_=bank[:].rearrange("p (k u i) -> p k i u", k=2, u=2, i=P),
                 )
+            if k < 4:
+                keep_busy(1)
 
         def quantise_pair(k):
             m, a = k // 4, k % 4

@@ -17,7 +17,6 @@ N = 1024
 D = 512
 FLOPS = 4 * 2 * N * N * D
 X_SPLIT = 88
-WARM_HEAD = 14
 
 
 def tile_simpa_pa_kernel(tc, A_p, A_n, x_n, w_n, out):
@@ -33,20 +32,13 @@ def tile_simpa_pa_kernel(tc, A_p, A_n, x_n, w_n, out):
             else:
                 nc.scalar.copy(out=dst, in_=src)
 
-        zeros = keep.tile([P, 512], BF16, name="zeros")
-        nc.vector.memset(zeros[:], 0.0)
-        warm = psum.tile([P, 512], F32, tag="mm", name="warm")
-
-        def keep_busy(times):
-            for i in range(times):
-                nc.tensor.matmul(out=warm[:], lhsT=zeros[:, 0:P], rhs=zeros[:], start=True, stop=True)
-
-        keep_busy(WARM_HEAD)
-
         ident = keep.tile([P, P], F32, name="ident")
         make_identity(nc, ident[:])
-        w_bf = keep.tile([P, 3], BF16, name="w_bf")
-        nc.scalar.dma_start(out=w_bf[:], in_=w_n.rearrange("a b -> (a b)").partition_broadcast(P))
+        w_row = keep.tile([P, 32], BF16, name="w_row")
+        nc.vector.memset(w_row[:], 0.0)
+        nc.scalar.dma_start(out=w_row[0:1, 0:3], in_=w_n.rearrange("a b -> b a"))
+        ones = keep.tile([P, P], BF16, name="ones")
+        nc.vector.memset(ones[:], 1.0)
 
         x_raw = keep.tile([P, 4096], BF16, name="x_raw")
         x_src = x_n.rearrange("(a p e) d -> p a (e d)", a=4, p=P, e=2)
@@ -60,8 +52,10 @@ def tile_simpa_pa_kernel(tc, A_p, A_n, x_n, w_n, out):
             nc.sync.dma_start(out=raw[:], in_=src[k % 4])
             a_raw.append(raw)
 
+        w_ps = psum.tile([P, 32], F32, tag="mm", name="w_ps")
+        nc.tensor.matmul(out=w_ps[:], lhsT=ones[:], rhs=w_row[:], start=True, stop=True)
         w_f = keep.tile([P, 3], F32, name="w_f")
-        nc.scalar.activation(out=w_f[:], in_=w_bf[:], func=COPY)
+        nc.scalar.activation(out=w_f[:], in_=w_ps[:, 0:3], func=COPY)
         wa = w_f[:, 0:1]
         wb = w_f[:, 1:2]
         wc = w_f[:, 2:3]
@@ -107,8 +101,6 @@ def tile_simpa_pa_kernel(tc, A_p, A_n, x_n, w_n, out):
                     out=grp_words[:, e * 512:(e + 1) * 512].rearrange("p (k i u) -> p k i u", k=2, i=P, u=2),
                     in_=bank[:].rearrange("p (k u i) -> p k i u", k=2, u=2, i=P),
                 )
-            if k < 4:
-                keep_busy(1)
 
         def quantise_pair(k):
             m, a = k // 4, k % 4

@@ -34,11 +34,8 @@ def tile_simpa_pa_kernel(tc, A_p, A_n, x_n, w_n, out):
 
         ident = keep.tile([P, P], F32, name="ident")
         make_identity(nc, ident[:])
-        w_row = keep.tile([P, 32], BF16, name="w_row")
-        nc.vector.memset(w_row[:], 0.0)
-        nc.scalar.dma_start(out=w_row[0:1, 0:3], in_=w_n.rearrange("a b -> b a"))
-        ones = keep.tile([P, P], BF16, name="ones")
-        nc.vector.memset(ones[:], 1.0)
+        w_bf = keep.tile([P, 3], BF16, name="w_bf")
+        nc.scalar.dma_start(out=w_bf[:], in_=w_n.rearrange("a b -> (a b)").partition_broadcast(P))
 
         x_raw = keep.tile([P, 4096], BF16, name="x_raw")
         x_src = x_n.rearrange("(a p e) d -> p a (e d)", a=4, p=P, e=2)
@@ -52,10 +49,8 @@ def tile_simpa_pa_kernel(tc, A_p, A_n, x_n, w_n, out):
             nc.sync.dma_start(out=raw[:], in_=src[k % 4])
             a_raw.append(raw)
 
-        w_ps = psum.tile([P, 32], F32, tag="mm", name="w_ps")
-        nc.tensor.matmul(out=w_ps[:], lhsT=ones[:], rhs=w_row[:], start=True, stop=True)
         w_f = keep.tile([P, 3], F32, name="w_f")
-        nc.scalar.activation(out=w_f[:], in_=w_ps[:, 0:3], func=COPY)
+        nc.gpsimd.tensor_copy(out=w_f[:], in_=w_bf[:])
         wa = w_f[:, 0:1]
         wb = w_f[:, 1:2]
         wc = w_f[:, 2:3]

from contextlib import ExitStack

import concourse.mybir as mybir
from concourse.masks import make_identity

F32 = mybir.dt.float32
BF16 = mybir.dt.bfloat16
U32 = mybir.dt.uint32
U8 = mybir.dt.uint8
FP8X4 = mybir.dt.float8_e4m3fn_x4
MULT = mybir.AluOpType.mult
ADD = mybir.AluOpType.add
COPY = mybir.ActivationFunctionType.Copy

P = 128
N = 1024
D = 512
FLOPS = 4 * 2 * N * N * D
X_SPLIT = 88


def tile_simpa_pa_kernel(tc, A_p, A_n, x_n, w_n, out):
    nc = tc.nc
    with ExitStack() as ctx:
        keep = ctx.enter_context(tc.tile_pool(name="keep", bufs=1))
        psum = ctx.enter_context(tc.psum_pool(name="psum", bufs=4))
        ctx.enter_context(tc.manual_schedule())

        def copy_on(on_vector, dst, src):
            if on_vector:
                nc.vector.tensor_copy(out=dst, in_=src)
            else:
                nc.scalar.copy(out=dst, in_=src)

        ident = keep.tile([P, P], F32, name="ident")
        make_identity(nc, ident[:])
        w_bf = keep.tile([P, 3], BF16, name="w_bf")
        nc.scalar.dma_start(out=w_bf[:], in_=w_n.rearrange("a b -> (a b)").partition_broadcast(P))

        x_raw = keep.tile([P, 4096], BF16, name="x_raw")
        x_src = x_n.rearrange("(a p e) d -> p a (e d)", a=4, p=P, e=2)
        x_dst = x_raw[:].rearrange("p (a f) -> p a f", a=4)
        for kg in range(2):
            nc.sync.dma_start(out=x_dst[:, 2 * kg:2 * kg + 2, :], in_=x_src[:, 2 * kg:2 * kg + 2, :])
        a_raw = []
        for k in range(8):
            src = (A_n, A_p)[k // 4].rearrange("(a p e) j -> a p (e j)", a=4, p=P, e=2)
            raw = keep.tile([P, 2048], BF16, name="a_raw%d" % k)
            nc.sync.dma_start(out=raw[:], in_=src[k % 4])
            a_raw.append(raw)

        w_f = keep.tile([P, 3], F32, name="w_f")
        nc.gpsimd.tensor_copy(out=w_f[:], in_=w_bf[:])
        wa = w_f[:, 0:1]
        wb = w_f[:, 1:2]
        wc = w_f[:, 2:3]

        x_grp = keep.tile([P, 4096], BF16, name="x_grp", align_bytes=64)
        x_cod = keep.tile([P, 1024], U32, name="x_cod", align_bytes=64)
        x_scl = keep.tile([P, 1024], U8, name="x_scl", align_bytes=64)
        for kg in range(2):
            dst = x_grp[:, kg * 2048:(kg + 1) * 2048].rearrange("p (c i t) -> p c t i", i=4, t=4)
            src = x_raw[:, kg * 2048:(kg + 1) * 2048].rearrange("p (t c i) -> p c t i", t=4, i=4)
            copy_on(True, dst[:, 0:X_SPLIT], src[:, 0:X_SPLIT])
            copy_on(False, dst[:, X_SPLIT:128], src[:, X_SPLIT:128])
        for kg in range(2):
            nc.vector.quantize_mx(
                out=x_cod[:, kg * 512:(kg + 1) * 512].bitcast(FP8X4),
                scales=x_scl[:, kg * 512:(kg + 1) * 512],
                in_=x_grp[:, kg * 2048:(kg + 1) * 2048],
            )

        a_cod = [keep.tile([P, 2048], U32, name="a_cod%d" % m, align_bytes=64) for m in range(2)]
        a_scl = [keep.tile([P, 2048], U8, name="a_scl%d" % m, align_bytes=64) for m in range(2)]
        h_grp = [keep.tile([P, 4096], BF16, name="h_grp%d" % m, align_bytes=64) for m in range(2)]
        h_cod = [keep.tile([P, 1024], U32, name="h_cod%d" % m, align_bytes=64) for m in range(2)]
        h_scl = [keep.tile([P, 1024], U8, name="h_scl%d" % m, align_bytes=64) for m in range(2)]
        acc = keep.tile([P, 4096], F32, name="acc")
        out_v = out.rearrange("(a p e) d -> a e p d", a=4, p=P, e=2)
        a_grp = {}

        def transpose_pair(k):
            words = a_raw[k][:].bitcast(F32)
            grp = keep.tile([P, 2048], BF16, name="a_grp%d" % k, align_bytes=64)
            a_grp[k] = grp
            grp_words = grp[:].bitcast(F32)
            for e in range(2):
                bank = psum.tile([P, 512], F32, tag="ts", name="tb%d%d" % (k, e))
                for s in range(4):
                    nc.tensor.transpose(
                        bank[:, s * P:(s + 1) * P],
                        words[:, e * 512 + s * P:e * 512 + (s + 1) * P],
                        ident[:],
                    )
                nc.scalar.copy(
                    out=grp_words[:, e * 512:(e + 1) * 512].rearrange("p (k i u) -> p k i u", k=2, i=P, u=2),
                    in_=bank[:].rearrange("p (k u i) -> p k i u", k=2, u=2, i=P),
                )

        def quantise_pair(k):
            m, a = k // 4, k % 4
            nc.vector.quantize_mx(
                out=a_cod[m][:, a * 512:(a + 1) * 512].bitcast(FP8X4),
                scales=a_scl[m][:, a * 512:(a + 1) * 512],
                in_=a_grp[k][:],
            )

        def mx(dst, m, r, kg, cod, scl, lo, hi):
            w0 = r * 256 + kg * P
            nc.tensor.matmul_mx(
                out=dst,
                lhsT=a_cod[m][:, w0:w0 + P].bitcast(FP8X4),
                lhsT_scale=a_scl[m][:, w0:w0 + P],
                rhs=cod[:, kg * 512 + lo:kg * 512 + hi].bitcast(FP8X4),
                rhs_scale=scl[:, kg * 512 + lo:kg * 512 + hi],
                start=(kg == 0),
                stop=(kg == 1),
            )

        def first_hop(m, g):
            banks = [psum.tile([P, 512], F32, tag="mm", name="mb%d%d%d" % (m, g, c)) for c in range(4)]
            for half in range(2):
                for c in range(4):
                    for t in (2 * half, 2 * half + 1):
                        for kg in range(2):
                            mx(banks[c][:, t * P:(t + 1) * P], m, 4 * g + t, kg, x_cod, x_scl, c * P, (c + 1) * P)
            return banks

        def evacuate(m, g, banks):
            for c in range(4):
                lo = g * 2048 + c * 512
                on_vector = c % 2 == 1
                copy_on(
                    on_vector,
                    h_grp[m][:, lo:lo + 512].rearrange("p (d t) -> p d t", t=4),
                    banks[c][:].rearrange("p (t d) -> p d t", t=4),
                )
                if m == 0:
                    dst = acc[:, g * 2048:(g + 1) * 2048].rearrange("p (t c d) -> p t c d", t=4, c=4)[:, :, c, :]
                    src = banks[c][:].rearrange("p (t d) -> p t d", t=4)
                    if on_vector:
                        nc.vector.tensor_scalar(out=dst, in0=src, scalar1=wa, scalar2=None, op0=MULT)
                    else:
                        nc.scalar.activation(out=dst, in_=src, func=COPY, scale=wa)
            nc.vector.quantize_mx(
                out=h_cod[m][:, g * 512:(g + 1) * 512].bitcast(FP8X4),
                scales=h_scl[m][:, g * 512:(g + 1) * 512],
                in_=h_grp[m][:, g * 2048:(g + 1) * 2048],
            )

        def second_hop(m, a, tag, weight, last):
            banks = []
            for e in range(2):
                bank = psum.tile([P, 512], F32, tag=tag, name="sb%d%d%d" % (m, a, e))
                for kg in range(2):
                    mx(bank[:], m, 2 * a + e, kg, h_cod[1 - m], h_scl[1 - m], 0, 512)
                banks.append(bank)
            for e in range(2):
                mine = acc[:, (2 * a + e) * 512:(2 * a + e + 1) * 512]
                if e == 0 and not last:
                    tmp = keep.tile([P, 512], F32, name="tmp%d" % a)
                    nc.scalar.activation(out=tmp[:], in_=banks[e][:], func=COPY, scale=weight)
                    nc.gpsimd.tensor_tensor(out=mine, in0=tmp[:], in1=mine, op=ADD)
                else:
                    nc.vector.scalar_tensor_tensor(
                        out=mine, in0=banks[e][:], scalar=weight, in1=mine, op0=MULT, op1=ADD
                    )
                if last:
                    nc.sync.dma_start(out=out_v[a, e], in_=mine)

        for k in (0, 1):
            transpose_pair(k)
        for k in (0, 1):
            quantise_pair(k)
        for i in range(4):
            m, g = i // 2, i % 2
            if i < 3:
                for k in (2 * i + 2, 2 * i + 3):
                    transpose_pair(k)
            else:
                second_hop(1, 0, "ts", wb, False)
                second_hop(1, 1, "ts", wb, False)
            banks = first_hop(m, g)
            if i < 3:
                for k in (2 * i + 2, 2 * i + 3):
                    quantise_pair(k)
            evacuate(m, g, banks)
        second_hop(1, 2, "ts", wb, False)
        second_hop(1, 3, "ts", wb, False)
        for a in range(4):
            second_hop(0, a, "mm" if a < 2 else "ts", wc, True)
